import numpy as np
import ml_dtypes

BF16 = ml_dtypes.bfloat16


def bf(x):
    return np.asarray(x, np.float32).astype(BF16)


def f32(x):
    return np.asarray(x, np.float32)


def f64(x):
    return np.asarray(x).astype(np.float64)


def striped(idx):
    return np.tile(idx.reshape(-1, 16).T, (8, 1))


S, D, M, N = 256, 128, 512, 512
W_GMF = 0.5


def setup_inputs():
    return {"items": bf(np.random.standard_normal((S, D))), "users": bf(np.random.standard_normal((D, M)) / np.sqrt(D)), "offs": striped(np.random.permutation(np.tile(np.arange(S), 2))[:N])}


def reference(items, users, offs):
    idx = offs[:16].T.reshape(-1)
    return W_GMF * (f64(users).T @ f64(items)[idx].T)

@@ -1,0 +1,57 @@
+import concourse.mybir as mybir
+from concourse.masks import make_identity
+
+P = 128
+SONGS = 256
+USERS = 512
+LIST = 512
+PIECE = 256
+PER_COLUMN = 16
+W_GMF = 0.5
+
+FLOPS = 2 * USERS * LIST * P
+
+BF16, F32, U16 = mybir.dt.bfloat16, mybir.dt.float32, mybir.dt.uint16
+
+
+def tile_modelncf_kernel(tc, items, users, offs, out):
+    nc = tc.nc
+    with (
+        tc.tile_pool(name="held", bufs=1) as held,
+        tc.tile_pool(name="staging", bufs=4) as staging,
+        tc.psum_pool(name="flip", bufs=1) as flip,
+        tc.psum_pool(name="banks", bufs=4) as banks,
+    ):
+        offsets = held.tile([P, LIST // PER_COLUMN], U16, name="offsets")
+        nc.sync.dma_start(offsets[:], offs)
+        song_rows = held.tile([P, SONGS // P, P], BF16, name="song_rows")
+        nc.sync.dma_start(song_rows[:], items.rearrange("(b p) d -> p b d", p=P))
+        users_sb = held.tile([P, USERS], BF16, name="users_sb")
+        nc.scalar.dma_start(users_sb[:], users)
+
+        identity = held.tile([P, P], BF16, name="identity")
+        make_identity(nc, identity[:])
+        flipped = flip.tile([P, SONGS], BF16, name="flipped")
+        for b in range(SONGS // P):
+            nc.tensor.transpose(flipped[:, b * P : (b + 1) * P], song_rows[:, b, :], identity[:])
+        window = held.tile([P, SONGS], BF16, name="window")
+        nc.vector.tensor_copy(window[:], flipped[:])
+
+        for u in range(USERS // P):
+            bank = banks.tile([P, LIST], F32, name="bank")
+            for c in range(LIST // PIECE):
+                k = PIECE // PER_COLUMN
+                nc.tensor.matmul(
+                    bank[:, c * PIECE : (c + 1) * PIECE],
+                    users_sb[:, u * P : (u + 1) * P],
+                    window[:].indirect(offsets[:, c * k : (c + 1) * k]),
+                    start=True,
+                    stop=True,
+                )
+            scored = staging.tile([P, LIST], F32, name="scored")
+            if u % 2 == 0:
+                nc.vector.tensor_scalar_mul(scored[:], bank[:], W_GMF)
+                nc.sync.dma_start(out[u * P : (u + 1) * P, :], scored[:])
+            else:
+                nc.scalar.mul(scored[:], bank[:], W_GMF)
+                nc.scalar.dma_start(out[u * P : (u + 1) * P, :], scored[:])

@@ -8,6 +8,7 @@ LIST = 512
 PIECE = 256
 PER_COLUMN = 16
 W_GMF = 0.5
+WARM_UPS = 5
 
 FLOPS = 2 * USERS * LIST * P
 
@@ -28,6 +29,12 @@ def tile_modelncf_kernel(tc, items, users, offs, out):
         nc.sync.dma_start(song_rows[:], items.rearrange("(b p) d -> p b d", p=P))
         users_sb = held.tile([P, USERS], BF16, name="users_sb")
         nc.scalar.dma_start(users_sb[:], users)
+
+        zeros = held.tile([P, LIST], BF16, name="zeros")
+        nc.vector.memset(zeros[:], 0.0)
+        unread = flip.tile([P, LIST], F32, name="unread")
+        for w in range(WARM_UPS):
+            nc.tensor.matmul(unread[:], zeros[:, :P], zeros[:], start=True, stop=True)
 
         identity = held.tile([P, P], BF16, name="identity")
         make_identity(nc, identity[:])

@@ -8,7 +8,7 @@ LIST = 512
 PIECE = 256
 PER_COLUMN = 16
 W_GMF = 0.5
-WARM_UPS = 5
+WARM_UPS = 20
 
 FLOPS = 2 * USERS * LIST * P
 
@@ -23,18 +23,18 @@ def tile_modelncf_kernel(tc, items, users, offs, out):
         tc.psum_pool(name="flip", bufs=1) as flip,
         tc.psum_pool(name="banks", bufs=4) as banks,
     ):
+        zeros = held.tile([P, P], BF16, name="zeros")
+        nc.gpsimd.memset(zeros[:], 0.0)
+        unread = flip.tile([P, P], F32, name="unread")
+        for w in range(WARM_UPS):
+            nc.tensor.matmul(unread[:], zeros[:], zeros[:], start=True, stop=True)
+
         offsets = held.tile([P, LIST // PER_COLUMN], U16, name="offsets")
         nc.sync.dma_start(offsets[:], offs)
         song_rows = held.tile([P, SONGS // P, P], BF16, name="song_rows")
         nc.sync.dma_start(song_rows[:], items.rearrange("(b p) d -> p b d", p=P))
         users_sb = held.tile([P, USERS], BF16, name="users_sb")
         nc.scalar.dma_start(users_sb[:], users)
-
-        zeros = held.tile([P, LIST], BF16, name="zeros")
-        nc.vector.memset(zeros[:], 0.0)
-        unread = flip.tile([P, LIST], F32, name="unread")
-        for w in range(WARM_UPS):
-            nc.tensor.matmul(unread[:], zeros[:, :P], zeros[:], start=True, stop=True)
 
         identity = held.tile([P, P], BF16, name="identity")
         make_identity(nc, identity[:])

@@ -8,7 +8,6 @@ LIST = 512
 PIECE = 256
 PER_COLUMN = 16
 W_GMF = 0.5
-WARM_UPS = 20
 
 FLOPS = 2 * USERS * LIST * P
 
@@ -19,16 +18,10 @@ def tile_modelncf_kernel(tc, items, users, offs, out):
     nc = tc.nc
     with (
         tc.tile_pool(name="held", bufs=1) as held,
-        tc.tile_pool(name="staging", bufs=4) as staging,
+        tc.tile_pool(name="staging", bufs=8) as staging,
         tc.psum_pool(name="flip", bufs=1) as flip,
-        tc.psum_pool(name="banks", bufs=4) as banks,
+        tc.psum_pool(name="banks", bufs=6) as banks,
     ):
-        zeros = held.tile([P, P], BF16, name="zeros")
-        nc.gpsimd.memset(zeros[:], 0.0)
-        unread = flip.tile([P, P], F32, name="unread")
-        for w in range(WARM_UPS):
-            nc.tensor.matmul(unread[:], zeros[:], zeros[:], start=True, stop=True)
-
         offsets = held.tile([P, LIST // PER_COLUMN], U16, name="offsets")
         nc.sync.dma_start(offsets[:], offs)
         song_rows = held.tile([P, SONGS // P, P], BF16, name="song_rows")
@@ -44,21 +37,20 @@ def tile_modelncf_kernel(tc, items, users, offs, out):
         window = held.tile([P, SONGS], BF16, name="window")
         nc.vector.tensor_copy(window[:], flipped[:])
 
+        k = PIECE // PER_COLUMN
         for u in range(USERS // P):
-            bank = banks.tile([P, LIST], F32, name="bank")
             for c in range(LIST // PIECE):
-                k = PIECE // PER_COLUMN
+                bank = banks.tile([P, PIECE], F32, name="bank")
                 nc.tensor.matmul(
-                    bank[:, c * PIECE : (c + 1) * PIECE],
+                    bank[:],
                     users_sb[:, u * P : (u + 1) * P],
                     window[:].indirect(offsets[:, c * k : (c + 1) * k]),
                     start=True,
                     stop=True,
                 )
-            scored = staging.tile([P, LIST], F32, name="scored")
-            if u % 2 == 0:
-                nc.vector.tensor_scalar_mul(scored[:], bank[:], W_GMF)
-                nc.sync.dma_start(out[u * P : (u + 1) * P, :], scored[:])
-            else:
-                nc.scalar.mul(scored[:], bank[:], W_GMF)
-                nc.scalar.dma_start(out[u * P : (u + 1) * P, :], scored[:])
+                scored = staging.tile([P, PIECE], F32, name="scored")
+                if c % 2 == 0:
+                    nc.vector.tensor_scalar_mul(scored[:], bank[:], W_GMF)
+                else:
+                    nc.scalar.mul(scored[:], bank[:], W_GMF)
+                nc.sync.dma_start(out[u * P : (u + 1) * P, c * PIECE : (c + 1) * PIECE], scored[:])

@@ -18,7 +18,7 @@ def tile_modelncf_kernel(tc, items, users, offs, out):
     nc = tc.nc
     with (
         tc.tile_pool(name="held", bufs=1) as held,
-        tc.tile_pool(name="staging", bufs=8) as staging,
+        tc.tile_pool(name="staging", bufs=4) as staging,
         tc.psum_pool(name="flip", bufs=1) as flip,
         tc.psum_pool(name="banks", bufs=6) as banks,
     ):
@@ -39,6 +39,7 @@ def tile_modelncf_kernel(tc, items, users, offs, out):
 
         k = PIECE // PER_COLUMN
         for u in range(USERS // P):
+            scored = staging.tile([P, LIST], F32, name="scored")
             for c in range(LIST // PIECE):
                 bank = banks.tile([P, PIECE], F32, name="bank")
                 nc.tensor.matmul(
@@ -48,9 +49,9 @@ def tile_modelncf_kernel(tc, items, users, offs, out):
                     start=True,
                     stop=True,
                 )
-                scored = staging.tile([P, PIECE], F32, name="scored")
                 if c % 2 == 0:
-                    nc.vector.tensor_scalar_mul(scored[:], bank[:], W_GMF)
+                    nc.vector.tensor_scalar_mul(scored[:, c * PIECE : (c + 1) * PIECE], bank[:], W_GMF)
                 else:
-                    nc.scalar.mul(scored[:], bank[:], W_GMF)
-                nc.sync.dma_start(out[u * P : (u + 1) * P, c * PIECE : (c + 1) * PIECE], scored[:])
+                    nc.scalar.mul(scored[:, c * PIECE : (c + 1) * PIECE], bank[:], W_GMF)
+            queue = nc.sync if u % 2 == 0 else nc.scalar
+            queue.dma_start(out[u * P : (u + 1) * P, :], scored[:])

@@ -22,12 +22,12 @@ def tile_modelncf_kernel(tc, items, users, offs, out):
         tc.psum_pool(name="flip", bufs=1) as flip,
         tc.psum_pool(name="banks", bufs=6) as banks,
     ):
-        offsets = held.tile([P, LIST // PER_COLUMN], U16, name="offsets")
-        nc.sync.dma_start(offsets[:], offs)
         song_rows = held.tile([P, SONGS // P, P], BF16, name="song_rows")
         nc.sync.dma_start(song_rows[:], items.rearrange("(b p) d -> p b d", p=P))
         users_sb = held.tile([P, USERS], BF16, name="users_sb")
         nc.scalar.dma_start(users_sb[:], users)
+        offsets = held.tile([P, LIST // PER_COLUMN], U16, name="offsets")
+        nc.sync.dma_start(offsets[:], offs)
 
         identity = held.tile([P, P], BF16, name="identity")
         make_identity(nc, identity[:])

@@ -49,9 +49,6 @@ def tile_modelncf_kernel(tc, items, users, offs, out):
                     start=True,
                     stop=True,
                 )
-                if c % 2 == 0:
-                    nc.vector.tensor_scalar_mul(scored[:, c * PIECE : (c + 1) * PIECE], bank[:], W_GMF)
-                else:
-                    nc.scalar.mul(scored[:, c * PIECE : (c + 1) * PIECE], bank[:], W_GMF)
+                nc.vector.tensor_scalar_mul(scored[:, c * PIECE : (c + 1) * PIECE], bank[:], W_GMF)
             queue = nc.sync if u % 2 == 0 else nc.scalar
             queue.dma_start(out[u * P : (u + 1) * P, :], scored[:])

@@ -50,5 +50,4 @@ def tile_modelncf_kernel(tc, items, users, offs, out):
                     stop=True,
                 )
                 nc.vector.tensor_scalar_mul(scored[:, c * PIECE : (c + 1) * PIECE], bank[:], W_GMF)
-            queue = nc.sync if u % 2 == 0 else nc.scalar
-            queue.dma_start(out[u * P : (u + 1) * P, :], scored[:])
+            nc.sync.dma_start(out[u * P : (u + 1) * P, :], scored[:])

@@ -50,4 +50,10 @@ def tile_modelncf_kernel(tc, items, users, offs, out):
                     stop=True,
                 )
                 nc.vector.tensor_scalar_mul(scored[:, c * PIECE : (c + 1) * PIECE], bank[:], W_GMF)
-            nc.sync.dma_start(out[u * P : (u + 1) * P, :], scored[:])
+                if u == 0:
+                    nc.sync.dma_start(
+                        out[u * P : (u + 1) * P, c * PIECE : (c + 1) * PIECE],
+                        scored[:, c * PIECE : (c + 1) * PIECE],
+                    )
+            if u != 0:
+                nc.sync.dma_start(out[u * P : (u + 1) * P, :], scored[:])

@@ -49,7 +49,10 @@ def tile_modelncf_kernel(tc, items, users, offs, out):
                     start=True,
                     stop=True,
                 )
-                nc.vector.tensor_scalar_mul(scored[:, c * PIECE : (c + 1) * PIECE], bank[:], W_GMF)
+                if c % 2 == 0:
+                    nc.vector.tensor_scalar_mul(scored[:, c * PIECE : (c + 1) * PIECE], bank[:], W_GMF)
+                else:
+                    nc.scalar.mul(scored[:, c * PIECE : (c + 1) * PIECE], bank[:], W_GMF)
                 if u == 0:
                     nc.sync.dma_start(
                         out[u * P : (u + 1) * P, c * PIECE : (c + 1) * PIECE],

@@ -20,7 +20,7 @@ def tile_modelncf_kernel(tc, items, users, offs, out):
         tc.tile_pool(name="held", bufs=1) as held,
         tc.tile_pool(name="staging", bufs=4) as staging,
         tc.psum_pool(name="flip", bufs=1) as flip,
-        tc.psum_pool(name="banks", bufs=6) as banks,
+        tc.psum_pool(name="banks", bufs=7) as banks,
     ):
         song_rows = held.tile([P, SONGS // P, P], BF16, name="song_rows")
         nc.sync.dma_start(song_rows[:], items.rearrange("(b p) d -> p b d", p=P))
@@ -37,26 +37,26 @@ def tile_modelncf_kernel(tc, items, users, offs, out):
         window = held.tile([P, SONGS], BF16, name="window")
         nc.vector.tensor_copy(window[:], flipped[:])
 
-        k = PIECE // PER_COLUMN
+        whole = [(0, PIECE), (PIECE, LIST)]
+        cut = [(0, PIECE), (PIECE, PIECE + PIECE // 2), (PIECE + PIECE // 2, LIST)]
+        filled = 0
         for u in range(USERS // P):
             scored = staging.tile([P, LIST], F32, name="scored")
-            for c in range(LIST // PIECE):
-                bank = banks.tile([P, PIECE], F32, name="bank")
+            for lo, hi in cut if u == USERS // P - 1 else whole:
+                bank = banks.tile([P, hi - lo], F32, name="bank")
                 nc.tensor.matmul(
                     bank[:],
                     users_sb[:, u * P : (u + 1) * P],
-                    window[:].indirect(offsets[:, c * k : (c + 1) * k]),
+                    window[:].indirect(offsets[:, lo // PER_COLUMN : hi // PER_COLUMN]),
                     start=True,
                     stop=True,
                 )
-                if c % 2 == 0:
-                    nc.vector.tensor_scalar_mul(scored[:, c * PIECE : (c + 1) * PIECE], bank[:], W_GMF)
+                if filled % 2 == 0:
+                    nc.vector.tensor_scalar_mul(scored[:, lo:hi], bank[:], W_GMF)
                 else:
-                    nc.scalar.mul(scored[:, c * PIECE : (c + 1) * PIECE], bank[:], W_GMF)
+                    nc.scalar.mul(scored[:, lo:hi], bank[:], W_GMF)
+                filled += 1
                 if u == 0:
-                    nc.sync.dma_start(
-                        out[u * P : (u + 1) * P, c * PIECE : (c + 1) * PIECE],
-                        scored[:, c * PIECE : (c + 1) * PIECE],
-                    )
+                    nc.sync.dma_start(out[u * P : (u + 1) * P, lo:hi], scored[:, lo:hi])
             if u != 0:
                 nc.sync.dma_start(out[u * P : (u + 1) * P, :], scored[:])

@@ -19,8 +19,7 @@ def tile_modelncf_kernel(tc, items, users, offs, out):
     with (
         tc.tile_pool(name="held", bufs=1) as held,
         tc.tile_pool(name="staging", bufs=4) as staging,
-        tc.psum_pool(name="flip", bufs=1) as flip,
-        tc.psum_pool(name="banks", bufs=7) as banks,
+        tc.psum_pool(name="banks", bufs=8) as banks,
     ):
         song_rows = held.tile([P, SONGS // P, P], BF16, name="song_rows")
         nc.sync.dma_start(song_rows[:], items.rearrange("(b p) d -> p b d", p=P))
@@ -31,11 +30,11 @@ def tile_modelncf_kernel(tc, items, users, offs, out):
 
         identity = held.tile([P, P], BF16, name="identity")
         make_identity(nc, identity[:])
-        flipped = flip.tile([P, SONGS], BF16, name="flipped")
-        for b in range(SONGS // P):
-            nc.tensor.transpose(flipped[:, b * P : (b + 1) * P], song_rows[:, b, :], identity[:])
         window = held.tile([P, SONGS], BF16, name="window")
-        nc.vector.tensor_copy(window[:], flipped[:])
+        for b in range(SONGS // P):
+            flipped = banks.tile([P, P], BF16, name="flipped", tag="bank")
+            nc.tensor.transpose(flipped[:], song_rows[:, b, :], identity[:])
+            nc.vector.tensor_copy(window[:, b * P : (b + 1) * P], flipped[:])
 
         whole = [(0, PIECE), (PIECE, LIST)]
         cut = [(0, PIECE), (PIECE, PIECE + PIECE // 2), (PIECE + PIECE // 2, LIST)]

import concourse.mybir as mybir
from concourse.masks import make_identity

P = 128
SONGS = 256
USERS = 512
LIST = 512
PIECE = 256
PER_COLUMN = 16
W_GMF = 0.5

FLOPS = 2 * USERS * LIST * P

BF16, F32, U16 = mybir.dt.bfloat16, mybir.dt.float32, mybir.dt.uint16


def tile_modelncf_kernel(tc, items, users, offs, out):
    nc = tc.nc
    with (
        tc.tile_pool(name="held", bufs=1) as held,
        tc.tile_pool(name="staging", bufs=4) as staging,
        tc.psum_pool(name="banks", bufs=8) as banks,
    ):
        song_rows = held.tile([P, SONGS // P, P], BF16, name="song_rows")
        nc.sync.dma_start(song_rows[:], items.rearrange("(b p) d -> p b d", p=P))
        users_sb = held.tile([P, USERS], BF16, name="users_sb")
        nc.scalar.dma_start(users_sb[:], users)
        offsets = held.tile([P, LIST // PER_COLUMN], U16, name="offsets")
        nc.sync.dma_start(offsets[:], offs)

        identity = held.tile([P, P], BF16, name="identity")
        make_identity(nc, identity[:])
        window = held.tile([P, SONGS], BF16, name="window")
        for b in range(SONGS // P):
            flipped = banks.tile([P, P], BF16, name="flipped", tag="bank")
            nc.tensor.transpose(flipped[:], song_rows[:, b, :], identity[:])
            nc.vector.tensor_copy(window[:, b * P : (b + 1) * P], flipped[:])

        whole = [(0, PIECE), (PIECE, LIST)]
        cut = [(0, PIECE), (PIECE, PIECE + PIECE // 2), (PIECE + PIECE // 2, LIST)]
        filled = 0
        for u in range(USERS // P):
            scored = staging.tile([P, LIST], F32, name="scored")
            for lo, hi in cut if u == USERS // P - 1 else whole:
                bank = banks.tile([P, hi - lo], F32, name="bank")
                nc.tensor.matmul(
                    bank[:],
                    users_sb[:, u * P : (u + 1) * P],
                    window[:].indirect(offsets[:, lo // PER_COLUMN : hi // PER_COLUMN]),
                    start=True,
                    stop=True,
                )
                if filled % 2 == 0:
                    nc.vector.tensor_scalar_mul(scored[:, lo:hi], bank[:], W_GMF)
                else:
                    nc.scalar.mul(scored[:, lo:hi], bank[:], W_GMF)
                filled += 1
                if u == 0:
                    nc.sync.dma_start(out[u * P : (u + 1) * P, lo:hi], scored[:, lo:hi])
            if u != 0:
                nc.sync.dma_start(out[u * P : (u + 1) * P, :], scored[:])
